import numpy as np
import ml_dtypes


def mxq(x, axis, fmt="e4m3"):
    dtype, down = {"e4m3": (ml_dtypes.float8_e4m3fn, 7), "e5m2": (ml_dtypes.float8_e5m2, 14)}[fmt]
    v = np.moveaxis(np.asarray(x, np.float32).astype(ml_dtypes.bfloat16).astype(np.float64), axis, -1)
    blocks = v.reshape(v.shape[:-1] + (-1, 32))
    amax = np.abs(blocks).max(-1, keepdims=True)
    byte = np.maximum(np.where(amax > 0, np.frexp(amax)[1] - 1 + 127, 0) - down, 1)
    scale = np.exp2(byte - 127.0)
    codes = (blocks / scale).astype(np.float32).astype(dtype).astype(np.float64)
    return np.moveaxis((codes * scale).reshape(v.shape), -1, axis)


WIDE = False


def mx_kscale(k):
    if not WIDE:
        return np.ones(k)
    levels = np.array([10, -10, 5, -5, 0])
    a = np.random.permutation(np.resize(levels, k // 512 * 4)).reshape(k // 512, 4)
    idx = np.arange(k)
    return np.exp2(a[idx // 512, idx % 128 // 32])


BF16 = ml_dtypes.bfloat16


def bf(x):
    return np.asarray(x, np.float32).astype(BF16)


def f64(x):
    return np.asarray(x).astype(np.float64)


B, CIN, H, W, COUT, N = 8, 1024, 32, 32, 256, 9


def setup_inputs():
    s = mx_kscale(CIN)
    return {"x": bf(np.random.standard_normal((B, CIN, H, W)) * s[None, :, None, None]),
            "weights": bf(np.random.standard_normal((N, COUT, CIN, 1, 1)) * np.sqrt(N) / np.sqrt(CIN) / s[None, None, :, None, None]),
            "biases": bf(np.random.standard_normal((N, COUT)) * 0.5 * np.sqrt(N))}


def reference(x, weights, biases):
    w = np.mean(f64(weights), axis=0)[:, :, 0, 0]
    b = np.mean(f64(biases), axis=0)
    y = np.einsum('bchw,oc->bohw', mxq(f64(x), 1, "e4m3"), mxq(w, 1, "e4m3"), optimize=True) + b[None, :, None, None]
    return y

@@ -1,0 +1,169 @@
+from contextlib import ExitStack
+
+import concourse.mybir as mybir
+from concourse.masks import make_identity
+
+F32 = mybir.dt.float32
+BF16 = mybir.dt.bfloat16
+U32 = mybir.dt.uint32
+U8 = mybir.dt.uint8
+FP8X4 = mybir.dt.float8_e4m3fn_x4
+ADD = mybir.AluOpType.add
+ACT = mybir.ActivationFunctionType
+
+P = 128
+PACK = 4
+K_PASS = P * PACK
+N_TILE = 512
+
+IMAGES, CIN, PIXELS, COUT, LAYERS = 8, 1024, 32 * 32, 256, 9
+PASSES = CIN // K_PASS
+O_BLOCKS = COUT // P
+PIXEL_TILES = PIXELS // N_TILE
+UNITS = IMAGES * PASSES
+
+RUN = 4
+VECTOR_RUNS = 160
+PREFETCH = 7
+
+FLOPS = 2 * IMAGES * PIXELS * CIN * COUT
+
+
+def tile_conv_1x1_9_layer_t_kernel(tc, x, weights, biases, out):
+    nc = tc.nc
+    w_rows = weights.rearrange("i (m b) c s t -> i m b (c s t)", b=O_BLOCKS)
+    y_rows = out.rearrange("n (m b) h v -> n m b (h v)", b=O_BLOCKS)
+
+    with ExitStack() as ctx:
+        const = ctx.enter_context(tc.tile_pool(name="const", bufs=1))
+        w_pool = ctx.enter_context(tc.tile_pool(name="w_pool", bufs=1))
+        raw_pool = ctx.enter_context(tc.tile_pool(name="raw_pool", bufs=PREFETCH + 1))
+        grouped_pool = ctx.enter_context(tc.tile_pool(name="grouped_pool", bufs=3))
+        code_pool = ctx.enter_context(tc.tile_pool(name="code_pool", bufs=4))
+        y_pool = ctx.enter_context(tc.tile_pool(name="y_pool", bufs=4))
+        psum = ctx.enter_context(tc.psum_pool(name="psum", bufs=8))
+
+        bias_rows = const.tile([P, COUT], BF16)
+        nc.vector.memset(bias_rows[:], 0.0)
+        nc.scalar.dma_start(out=bias_rows[0:LAYERS, :], in_=biases)
+
+        w_layers = []
+        for i in range(LAYERS):
+            w_layer = w_pool.tile([P, O_BLOCKS, CIN], BF16, name="w_layer%d" % i)
+            nc.sync.dma_start(out=w_layer[:], in_=w_rows[i])
+            w_layers.append(w_layer)
+
+        x_raw = {}
+
+        def load_unit(u):
+            n, g = divmod(u, PASSES)
+            raw = raw_pool.tile([P, PACK, PIXELS], BF16, name="raw")
+            rows = x[n].rearrange("(g p j) h v -> g p j (h v)", g=PASSES, p=P, j=PACK)
+            nc.sync.dma_start(out=raw[:], in_=rows[g])
+            x_raw[u] = raw
+
+        for u in range(PREFETCH):
+            load_unit(u)
+
+        ident = const.tile([P, P], F32)
+        make_identity(nc, ident[:])
+
+        bias_t = psum.tile([P, P], F32, tag="bank")
+        nc.tensor.transpose(bias_t[:], bias_rows[:].bitcast(F32), ident[:])
+        bias_sum = const.tile([P, O_BLOCKS], F32)
+        nc.vector.tensor_reduce(
+            out=bias_sum[:],
+            in_=bias_t[:].bitcast(BF16).rearrange("m (i b) -> m b i", b=O_BLOCKS)[:, :, 0:LAYERS],
+            axis=mybir.AxisListType.X,
+            op=ADD,
+        )
+        bias_mean = const.tile([P, O_BLOCKS], F32)
+        nc.vector.tensor_scalar_mul(out=bias_mean[:], in0=bias_sum[:], scalar1=1.0 / LAYERS)
+
+        w_sum = w_pool.tile([P, O_BLOCKS, CIN], F32)
+        for i in range(1, LAYERS):
+            for b in range(O_BLOCKS):
+                so_far = w_layers[0] if i == 1 else w_sum
+                nc.vector.tensor_tensor(
+                    out=w_sum[:, b, :], in0=so_far[:, b, :], in1=w_layers[i][:, b, :], op=ADD
+                )
+        w_mean = w_pool.tile([P, O_BLOCKS, CIN], BF16)
+        for b in range(O_BLOCKS):
+            nc.scalar.activation(
+                out=w_mean[:, b, :], in_=w_sum[:, b, :], func=ACT.Copy, scale=1.0 / LAYERS
+            )
+
+        w_grouped = w_pool.tile([P, PASSES * O_BLOCKS * P * PACK], BF16, align_bytes=64)
+        w_grouped_words = w_grouped[:].bitcast(F32).rearrange(
+            "p (g b m e) -> p g b m e", g=PASSES, b=O_BLOCKS, e=PACK // 2
+        )
+        words_per_pass = K_PASS // 2
+        for g in range(PASSES):
+            w_t = psum.tile([P, O_BLOCKS, PACK // 2, P], F32, tag="bank")
+            for b in range(O_BLOCKS):
+                words = w_mean[:, b, :].bitcast(F32)
+                for e in range(PACK // 2):
+                    nc.tensor.transpose(
+                        w_t[:, b, e, :],
+                        words[:, g * words_per_pass + e : (g + 1) * words_per_pass : PACK // 2],
+                        ident[:],
+                    )
+            nc.scalar.copy(out=w_grouped_words[:, g], in_=w_t[:].rearrange("p b e m -> p b m e"))
+        w_codes = w_pool.tile([P, PASSES * O_BLOCKS * P], U32, align_bytes=64)
+        w_scales = w_pool.tile([P, PASSES * O_BLOCKS * P], U8, align_bytes=64)
+        nc.vector.quantize_mx(out=w_codes[:].bitcast(FP8X4), scales=w_scales[:], in_=w_grouped[:])
+
+        x_grouped = {}
+        x_codes = {}
+        x_scales = {}
+
+        def regroup_unit(u):
+            grouped = grouped_pool.tile([P, PIXELS, PACK], BF16, name="grouped", align_bytes=64)
+            src = x_raw[u][:].rearrange("p j (r i) -> p r j i", i=RUN)
+            dst = grouped[:].rearrange("p (r i) j -> p r j i", i=RUN)
+            nc.vector.tensor_copy(out=dst[:, 0:VECTOR_RUNS], in_=src[:, 0:VECTOR_RUNS])
+            nc.scalar.copy(out=dst[:, VECTOR_RUNS:], in_=src[:, VECTOR_RUNS:])
+            x_grouped[u] = grouped
+
+        def quantise_unit(u):
+            n, g = divmod(u, PASSES)
+            if g == 0:
+                x_codes[n] = code_pool.tile([P, PASSES, PIXELS], U32, name="codes", align_bytes=64)
+                x_scales[n] = code_pool.tile([P, PASSES, PIXELS], U8, name="scales", align_bytes=64)
+            nc.vector.quantize_mx(
+                out=x_codes[n][:, g, :].bitcast(FP8X4),
+                scales=x_scales[n][:, g, :],
+                in_=x_grouped[u][:].rearrange("p w j -> p (w j)"),
+            )
+
+        def multiply_image(n):
+            y = y_pool.tile([P, O_BLOCKS, PIXELS], F32, name="y")
+            for b in range(O_BLOCKS):
+                for t in range(PIXEL_TILES):
+                    pixels = slice(t * N_TILE, (t + 1) * N_TILE)
+                    acc = psum.tile([P, N_TILE], F32, tag="bank")
+                    for g in range(PASSES):
+                        o_cols = slice((g * O_BLOCKS + b) * P, (g * O_BLOCKS + b + 1) * P)
+                        nc.tensor.matmul_mx(
+                            out=acc[:],
+                            lhsT=w_codes[:, o_cols].bitcast(FP8X4),
+                            lhsT_scale=w_scales[:, o_cols],
+                            rhs=x_codes[n][:, g, pixels].bitcast(FP8X4),
+                            rhs_scale=x_scales[n][:, g, pixels],
+                            start=(g == 0),
+                            stop=(g == PASSES - 1),
+                        )
+                    nc.scalar.activation(
+                        out=y[:, b, pixels], in_=acc[:], func=ACT.Identity, bias=bias_mean[:, b : b + 1]
+                    )
+            nc.sync.dma_start(out=y_rows[n], in_=y[:])
+
+        for u in range(UNITS + 1):
+            if u + PREFETCH < UNITS:
+                load_unit(u + PREFETCH)
+            if u < UNITS:
+                regroup_unit(u)
+            if u >= 1:
+                quantise_unit(u - 1)
+                if u % PASSES == 0:
+                    multiply_image(u // PASSES - 1)

@@ -24,6 +24,7 @@ UNITS = IMAGES * PASSES
 
 RUN = 4
 VECTOR_RUNS = 160
+VECTOR_LAYERS = 3
 PREFETCH = 7
 
 FLOPS = 2 * IMAGES * PIXELS * CIN * COUT
@@ -67,6 +68,8 @@ def tile_conv_1x1_9_layer_t_kernel(tc, x, weights, biases, out):
 
         ident = const.tile([P, P], F32)
         make_identity(nc, ident[:])
+        ident_bf = const.tile([P, P], BF16)
+        make_identity(nc, ident_bf[:])
 
         bias_t = psum.tile([P, P], F32, tag="bank")
         nc.tensor.transpose(bias_t[:], bias_rows[:].bitcast(F32), ident[:])
@@ -81,11 +84,31 @@ def tile_conv_1x1_9_layer_t_kernel(tc, x, weights, biases, out):
         nc.vector.tensor_scalar_mul(out=bias_mean[:], in0=bias_sum[:], scalar1=1.0 / LAYERS)
 
         w_sum = w_pool.tile([P, O_BLOCKS, CIN], F32)
-        for i in range(1, LAYERS):
+        for i in range(1, VECTOR_LAYERS):
             for b in range(O_BLOCKS):
                 so_far = w_layers[0] if i == 1 else w_sum
                 nc.vector.tensor_tensor(
                     out=w_sum[:, b, :], in0=so_far[:, b, :], in1=w_layers[i][:, b, :], op=ADD
+                )
+        c_tiles = CIN // N_TILE
+        w_banks = {}
+        for i in range(VECTOR_LAYERS, LAYERS):
+            for b in range(O_BLOCKS):
+                for h in range(c_tiles):
+                    if i == VECTOR_LAYERS:
+                        w_banks[b, h] = psum.tile([P, N_TILE], F32, tag="bank", name="w_bank")
+                    nc.tensor.matmul(
+                        out=w_banks[b, h][:],
+                        lhsT=ident_bf[:],
+                        rhs=w_layers[i][:, b, h * N_TILE : (h + 1) * N_TILE],
+                        start=(i == VECTOR_LAYERS),
+                        stop=(i == LAYERS - 1),
+                    )
+        for b in range(O_BLOCKS):
+            for h in range(c_tiles):
+                channels = slice(h * N_TILE, (h + 1) * N_TILE)
+                nc.vector.tensor_tensor(
+                    out=w_sum[:, b, channels], in0=w_banks[b, h][:], in1=w_sum[:, b, channels], op=ADD
                 )
         w_mean = w_pool.tile([P, O_BLOCKS, CIN], BF16)
         for b in range(O_BLOCKS):

@@ -21,40 +21,37 @@ PASSES = CIN // K_PASS
 O_BLOCKS = COUT // P
 PIXEL_TILES = PIXELS // N_TILE
 UNITS = IMAGES * PASSES
+WORDS = PACK // 2
 
 RUN = 4
-VECTOR_RUNS = 160
+VECTOR_RUNS = 168
 VECTOR_LAYERS = 3
-PREFETCH = 7
+RAW_BUFS = 12
+Y_BUFS = 12
+EMPTY_LAG = 3
 
 FLOPS = 2 * IMAGES * PIXELS * CIN * COUT
 
 
 def tile_conv_1x1_9_layer_t_kernel(tc, x, weights, biases, out):
     nc = tc.nc
+    assert O_BLOCKS == PASSES
     w_rows = weights.rearrange("i (m b) c s t -> i m b (c s t)", b=O_BLOCKS)
-    y_rows = out.rearrange("n (m b) h v -> n m b (h v)", b=O_BLOCKS)
+    y_rows = out.rearrange("n (m b) h v -> n b m (h v)", b=O_BLOCKS)
 
     with ExitStack() as ctx:
+        ctx.enter_context(tc.manual_schedule())
         const = ctx.enter_context(tc.tile_pool(name="const", bufs=1))
-        w_pool = ctx.enter_context(tc.tile_pool(name="w_pool", bufs=1))
-        raw_pool = ctx.enter_context(tc.tile_pool(name="raw_pool", bufs=PREFETCH + 1))
+        raw_pool = ctx.enter_context(tc.tile_pool(name="raw_pool", bufs=RAW_BUFS))
         grouped_pool = ctx.enter_context(tc.tile_pool(name="grouped_pool", bufs=3))
-        code_pool = ctx.enter_context(tc.tile_pool(name="code_pool", bufs=4))
-        y_pool = ctx.enter_context(tc.tile_pool(name="y_pool", bufs=4))
+        code_pool = ctx.enter_context(tc.tile_pool(name="code_pool", bufs=3))
         psum = ctx.enter_context(tc.psum_pool(name="psum", bufs=8))
 
-        bias_rows = const.tile([P, COUT], BF16)
-        nc.vector.memset(bias_rows[:], 0.0)
-        nc.scalar.dma_start(out=bias_rows[0:LAYERS, :], in_=biases)
-
-        w_layers = []
-        for i in range(LAYERS):
-            w_layer = w_pool.tile([P, O_BLOCKS, CIN], BF16, name="w_layer%d" % i)
-            nc.sync.dma_start(out=w_layer[:], in_=w_rows[i])
-            w_layers.append(w_layer)
-
         x_raw = {}
+        x_grouped = {}
+        x_codes = {}
+        x_scales = {}
+        banks = {}
 
         def load_unit(u):
             n, g = divmod(u, PASSES)
@@ -63,83 +60,6 @@ def tile_conv_1x1_9_layer_t_kernel(tc, x, weights, biases, out):
             nc.sync.dma_start(out=raw[:], in_=rows[g])
             x_raw[u] = raw
 
-        for u in range(PREFETCH):
-            load_unit(u)
-
-        ident = const.tile([P, P], F32)
-        make_identity(nc, ident[:])
-        ident_bf = const.tile([P, P], BF16)
-        make_identity(nc, ident_bf[:])
-
-        bias_t = psum.tile([P, P], F32, tag="bank")
-        nc.tensor.transpose(bias_t[:], bias_rows[:].bitcast(F32), ident[:])
-        bias_sum = const.tile([P, O_BLOCKS], F32)
-        nc.vector.tensor_reduce(
-            out=bias_sum[:],
-            in_=bias_t[:].bitcast(BF16).rearrange("m (i b) -> m b i", b=O_BLOCKS)[:, :, 0:LAYERS],
-            axis=mybir.AxisListType.X,
-            op=ADD,
-        )
-        bias_mean = const.tile([P, O_BLOCKS], F32)
-        nc.vector.tensor_scalar_mul(out=bias_mean[:], in0=bias_sum[:], scalar1=1.0 / LAYERS)
-
-        w_sum = w_pool.tile([P, O_BLOCKS, CIN], F32)
-        for i in range(1, VECTOR_LAYERS):
-            for b in range(O_BLOCKS):
-                so_far = w_layers[0] if i == 1 else w_sum
-                nc.vector.tensor_tensor(
-                    out=w_sum[:, b, :], in0=so_far[:, b, :], in1=w_layers[i][:, b, :], op=ADD
-                )
-        c_tiles = CIN // N_TILE
-        w_banks = {}
-        for i in range(VECTOR_LAYERS, LAYERS):
-            for b in range(O_BLOCKS):
-                for h in range(c_tiles):
-                    if i == VECTOR_LAYERS:
-                        w_banks[b, h] = psum.tile([P, N_TILE], F32, tag="bank", name="w_bank")
-                    nc.tensor.matmul(
-                        out=w_banks[b, h][:],
-                        lhsT=ident_bf[:],
-                        rhs=w_layers[i][:, b, h * N_TILE : (h + 1) * N_TILE],
-                        start=(i == VECTOR_LAYERS),
-                        stop=(i == LAYERS - 1),
-                    )
-        for b in range(O_BLOCKS):
-            for h in range(c_tiles):
-                channels = slice(h * N_TILE, (h + 1) * N_TILE)
-                nc.vector.tensor_tensor(
-                    out=w_sum[:, b, channels], in0=w_banks[b, h][:], in1=w_sum[:, b, channels], op=ADD
-                )
-        w_mean = w_pool.tile([P, O_BLOCKS, CIN], BF16)
-        for b in range(O_BLOCKS):
-            nc.scalar.activation(
-                out=w_mean[:, b, :], in_=w_sum[:, b, :], func=ACT.Copy, scale=1.0 / LAYERS
-            )
-
-        w_grouped = w_pool.tile([P, PASSES * O_BLOCKS * P * PACK], BF16, align_bytes=64)
-        w_grouped_words = w_grouped[:].bitcast(F32).rearrange(
-            "p (g b m e) -> p g b m e", g=PASSES, b=O_BLOCKS, e=PACK // 2
-        )
-        words_per_pass = K_PASS // 2
-        for g in range(PASSES):
-            w_t = psum.tile([P, O_BLOCKS, PACK // 2, P], F32, tag="bank")
-            for b in range(O_BLOCKS):
-                words = w_mean[:, b, :].bitcast(F32)
-                for e in range(PACK // 2):
-                    nc.tensor.transpose(
-                        w_t[:, b, e, :],
-                        words[:, g * words_per_pass + e : (g + 1) * words_per_pass : PACK // 2],
-                        ident[:],
-                    )
-            nc.scalar.copy(out=w_grouped_words[:, g], in_=w_t[:].rearrange("p b e m -> p b m e"))
-        w_codes = w_pool.tile([P, PASSES * O_BLOCKS * P], U32, align_bytes=64)
-        w_scales = w_pool.tile([P, PASSES * O_BLOCKS * P], U8, align_bytes=64)
-        nc.vector.quantize_mx(out=w_codes[:].bitcast(FP8X4), scales=w_scales[:], in_=w_grouped[:])
-
-        x_grouped = {}
-        x_codes = {}
-        x_scales = {}
-
         def regroup_unit(u):
             grouped = grouped_pool.tile([P, PIXELS, PACK], BF16, name="grouped", align_bytes=64)
             src = x_raw[u][:].rearrange("p j (r i) -> p r j i", i=RUN)
@@ -147,6 +67,8 @@ def tile_conv_1x1_9_layer_t_kernel(tc, x, weights, biases, out):
             nc.vector.tensor_copy(out=dst[:, 0:VECTOR_RUNS], in_=src[:, 0:VECTOR_RUNS])
             nc.scalar.copy(out=dst[:, VECTOR_RUNS:], in_=src[:, VECTOR_RUNS:])
             x_grouped[u] = grouped
+            if u + RAW_BUFS < UNITS:
+                load_unit(u + RAW_BUFS)
 
         def quantise_unit(u):
             n, g = divmod(u, PASSES)
@@ -159,34 +81,127 @@ def tile_conv_1x1_9_layer_t_kernel(tc, x, weights, biases, out):
                 in_=x_grouped[u][:].rearrange("p w j -> p (w j)"),
             )
 
-        def multiply_image(n):
-            y = y_pool.tile([P, O_BLOCKS, PIXELS], F32, name="y")
+        def multiply_unit(u):
+            n, g = divmod(u, PASSES)
             for b in range(O_BLOCKS):
+                o_cols = slice((g * O_BLOCKS + b) * P, (g * O_BLOCKS + b + 1) * P)
                 for t in range(PIXEL_TILES):
                     pixels = slice(t * N_TILE, (t + 1) * N_TILE)
-                    acc = psum.tile([P, N_TILE], F32, tag="bank")
-                    for g in range(PASSES):
-                        o_cols = slice((g * O_BLOCKS + b) * P, (g * O_BLOCKS + b + 1) * P)
-                        nc.tensor.matmul_mx(
-                            out=acc[:],
-                            lhsT=w_codes[:, o_cols].bitcast(FP8X4),
-                            lhsT_scale=w_scales[:, o_cols],
-                            rhs=x_codes[n][:, g, pixels].bitcast(FP8X4),
-                            rhs_scale=x_scales[n][:, g, pixels],
-                            start=(g == 0),
-                            stop=(g == PASSES - 1),
-                        )
-                    nc.scalar.activation(
-                        out=y[:, b, pixels], in_=acc[:], func=ACT.Identity, bias=bias_mean[:, b : b + 1]
+                    if g == 0:
+                        banks[n, b, t] = psum.tile([P, N_TILE], F32, tag="bank", name="acc")
+                    nc.tensor.matmul_mx(
+                        out=banks[n, b, t][:],
+                        lhsT=w_codes[:, o_cols].bitcast(FP8X4),
+                        lhsT_scale=w_scales[:, o_cols],
+                        rhs=x_codes[n][:, g, pixels].bitcast(FP8X4),
+                        rhs_scale=x_scales[n][:, g, pixels],
+                        start=(g == 0),
+                        stop=(g == PASSES - 1),
                     )
-            nc.sync.dma_start(out=y_rows[n], in_=y[:])
 
-        for u in range(UNITS + 1):
-            if u + PREFETCH < UNITS:
-                load_unit(u + PREFETCH)
+        def empty_block(s):
+            n, b = divmod(s, O_BLOCKS)
+            y = y_pool.tile([P, PIXELS], F32, name="y")
+            for t in range(PIXEL_TILES):
+                nc.scalar.activation(
+                    out=y[:, t * N_TILE : (t + 1) * N_TILE],
+                    in_=banks[n, b, t][:],
+                    func=ACT.Identity,
+                    bias=bias_mean[:, b : b + 1],
+                )
+            nc.sync.dma_start(out=y_rows[n, b], in_=y[:])
+
+        bias_rows = const.tile([P, COUT], BF16)
+        nc.vector.memset(bias_rows[:], 0.0)
+        nc.scalar.dma_start(out=bias_rows[0:LAYERS, :], in_=biases)
+        ident = const.tile([P, P], F32)
+        make_identity(nc, ident[:])
+        ident_bf = const.tile([P, P], BF16)
+        make_identity(nc, ident_bf[:])
+        w_codes = const.tile([P, PASSES * O_BLOCKS * P], U32, align_bytes=64)
+        w_scales = const.tile([P, PASSES * O_BLOCKS * P], U8, align_bytes=64)
+
+        with tc.tile_pool(name="w_pool", bufs=1) as w_pool:
+            w_layers = []
+            for i in range(LAYERS):
+                w_layer = w_pool.tile([P, O_BLOCKS, CIN], BF16, name="w_layer%d" % i)
+                nc.sync.dma_start(out=w_layer[:], in_=w_rows[i])
+                w_layers.append(w_layer)
+            for u in range(RAW_BUFS):
+                load_unit(u)
+
+            bias_t = psum.tile([P, P], F32, tag="bank")
+            nc.tensor.transpose(bias_t[:], bias_rows[:].bitcast(F32), ident[:])
+            bias_sum = const.tile([P, O_BLOCKS], F32)
+            nc.vector.tensor_reduce(
+                out=bias_sum[:],
+                in_=bias_t[:].bitcast(BF16).rearrange("m (i b) -> m b i", b=O_BLOCKS)[:, :, 0:LAYERS],
+                axis=mybir.AxisListType.X,
+                op=ADD,
+            )
+            bias_mean = const.tile([P, O_BLOCKS], F32)
+            nc.vector.tensor_scalar_mul(out=bias_mean[:], in0=bias_sum[:], scalar1=1.0 / LAYERS)
+
+            w_sum = w_pool.tile([P, O_BLOCKS, CIN], F32)
+            for i in range(1, VECTOR_LAYERS):
+                for b in range(O_BLOCKS):
+                    so_far = w_layers[0] if i == 1 else w_sum
+                    nc.vector.tensor_tensor(
+                        out=w_sum[:, b, :], in0=so_far[:, b, :], in1=w_layers[i][:, b, :], op=ADD
+                    )
+            w_banks = {}
+            for i in range(VECTOR_LAYERS, LAYERS):
+                for g in range(PASSES):
+                    for b in range(O_BLOCKS):
+                        if i == VECTOR_LAYERS:
+                            w_banks[g, b] = psum.tile([P, K_PASS], F32, tag="bank", name="w_bank")
+                        nc.tensor.matmul(
+                            out=w_banks[g, b][:],
+                            lhsT=ident_bf[:],
+                            rhs=w_layers[i][:, b, g * K_PASS : (g + 1) * K_PASS],
+                            start=(i == VECTOR_LAYERS),
+                            stop=(i == LAYERS - 1),
+                        )
+            w_mean = w_pool.tile([P, O_BLOCKS, CIN], BF16)
+            for g in range(PASSES):
+                for b in range(O_BLOCKS):
+                    channels = slice(g * K_PASS, (g + 1) * K_PASS)
+                    nc.vector.tensor_tensor(
+                        out=w_sum[:, b, channels], in0=w_banks[g, b][:], in1=w_sum[:, b, channels], op=ADD
+                    )
+                    nc.scalar.activation(
+                        out=w_mean[:, b, channels], in_=w_sum[:, b, channels], func=ACT.Copy, scale=1.0 / LAYERS
+                    )
+
+            regroup_unit(0)
+
+            w_grouped = w_pool.tile([P, PASSES * O_BLOCKS * P * PACK], BF16, align_bytes=64)
+            w_grouped_words = w_grouped[:].bitcast(F32).rearrange(
+                "p (g b m e) -> p g b m e", g=PASSES, b=O_BLOCKS, e=WORDS
+            )
+            pass_words = K_PASS // 2
+            for g in range(PASSES):
+                w_t = psum.tile([P, O_BLOCKS, WORDS, P], F32, tag="bank")
+                for b in range(O_BLOCKS):
+                    words = w_mean[:, b, :].bitcast(F32)
+                    for e in range(WORDS):
+                        nc.tensor.transpose(
+                            w_t[:, b, e, :], words[:, g * pass_words + e : (g + 1) * pass_words : WORDS], ident[:]
+                        )
+                nc.scalar.copy(out=w_grouped_words[:, g], in_=w_t[:].rearrange("p b e m -> p b m e"))
+
+            regroup_unit(1)
+            quantise_unit(0)
+            nc.vector.quantize_mx(out=w_codes[:].bitcast(FP8X4), scales=w_scales[:], in_=w_grouped[:])
+            multiply_unit(0)
+
+        y_pool = ctx.enter_context(tc.tile_pool(name="y_pool", bufs=Y_BUFS))
+
+        for u in range(2, UNITS + EMPTY_LAG):
             if u < UNITS:
                 regroup_unit(u)
-            if u >= 1:
+            if u - 1 < UNITS:
                 quantise_unit(u - 1)
-                if u % PASSES == 0:
-                    multiply_image(u // PASSES - 1)
+                multiply_unit(u - 1)
+            if u >= EMPTY_LAG:
+                empty_block(u - EMPTY_LAG)

@@ -130,18 +130,6 @@ def tile_conv_1x1_9_layer_t_kernel(tc, x, weights, biases, out):
             for u in range(RAW_BUFS):
                 load_unit(u)
 
-            bias_t = psum.tile([P, P], F32, tag="bank")
-            nc.tensor.transpose(bias_t[:], bias_rows[:].bitcast(F32), ident[:])
-            bias_sum = const.tile([P, O_BLOCKS], F32)
-            nc.vector.tensor_reduce(
-                out=bias_sum[:],
-                in_=bias_t[:].bitcast(BF16).rearrange("m (i b) -> m b i", b=O_BLOCKS)[:, :, 0:LAYERS],
-                axis=mybir.AxisListType.X,
-                op=ADD,
-            )
-            bias_mean = const.tile([P, O_BLOCKS], F32)
-            nc.vector.tensor_scalar_mul(out=bias_mean[:], in0=bias_sum[:], scalar1=1.0 / LAYERS)
-
             w_sum = w_pool.tile([P, O_BLOCKS, CIN], F32)
             for i in range(1, VECTOR_LAYERS):
                 for b in range(O_BLOCKS):
@@ -193,6 +181,18 @@ def tile_conv_1x1_9_layer_t_kernel(tc, x, weights, biases, out):
             regroup_unit(1)
             quantise_unit(0)
             nc.vector.quantize_mx(out=w_codes[:].bitcast(FP8X4), scales=w_scales[:], in_=w_grouped[:])
+            bias_t = psum.tile([P, P], F32, tag="bank")
+            nc.tensor.transpose(bias_t[:], bias_rows[:].bitcast(F32), ident[:])
+            bias_sum = const.tile([P, O_BLOCKS], F32)
+            nc.vector.tensor_reduce(
+                out=bias_sum[:],
+                in_=bias_t[:].bitcast(BF16).rearrange("m (i b) -> m b i", b=O_BLOCKS)[:, :, 0:LAYERS],
+                axis=mybir.AxisListType.X,
+                op=ADD,
+            )
+            bias_mean = const.tile([P, O_BLOCKS], F32)
+            nc.vector.tensor_scalar_mul(out=bias_mean[:], in0=bias_sum[:], scalar1=1.0 / LAYERS)
+
             multiply_unit(0)
 
         y_pool = ctx.enter_context(tc.tile_pool(name="y_pool", bufs=Y_BUFS))

@@ -70,23 +70,24 @@ def tile_conv_1x1_9_layer_t_kernel(tc, x, weights, biases, out):
             if u + RAW_BUFS < UNITS:
                 load_unit(u + RAW_BUFS)
 
-        def quantise_unit(u):
+        def quantise_unit(u, first_pixel=0, pixel_count=PIXELS):
             n, g = divmod(u, PASSES)
             if g == 0:
                 x_codes[n] = code_pool.tile([P, PASSES, PIXELS], U32, name="codes", align_bytes=64)
                 x_scales[n] = code_pool.tile([P, PASSES, PIXELS], U8, name="scales", align_bytes=64)
+            pixels = slice(first_pixel, first_pixel + pixel_count)
             nc.vector.quantize_mx(
-                out=x_codes[n][:, g, :].bitcast(FP8X4),
-                scales=x_scales[n][:, g, :],
-                in_=x_grouped[u][:].rearrange("p w j -> p (w j)"),
+                out=x_codes[n][:, g, pixels].bitcast(FP8X4),
+                scales=x_scales[n][:, g, pixels],
+                in_=x_grouped[u][:, pixels, :].rearrange("p w j -> p (w j)"),
             )
 
-        def multiply_unit(u):
+        def multiply_unit(u, pixel_tiles=range(PIXEL_TILES)):
             n, g = divmod(u, PASSES)
-            for b in range(O_BLOCKS):
-                o_cols = slice((g * O_BLOCKS + b) * P, (g * O_BLOCKS + b + 1) * P)
-                for t in range(PIXEL_TILES):
-                    pixels = slice(t * N_TILE, (t + 1) * N_TILE)
+            for t in pixel_tiles:
+                pixels = slice(t * N_TILE, (t + 1) * N_TILE)
+                for b in range(O_BLOCKS):
+                    o_cols = slice((g * O_BLOCKS + b) * P, (g * O_BLOCKS + b + 1) * P)
                     if g == 0:
                         banks[n, b, t] = psum.tile([P, N_TILE], F32, tag="bank", name="acc")
                     nc.tensor.matmul_mx(
@@ -99,16 +100,23 @@ def tile_conv_1x1_9_layer_t_kernel(tc, x, weights, biases, out):
                         stop=(g == PASSES - 1),
                     )
 
-        def empty_block(s):
+        def empty_block(s, on_vector=False):
             n, b = divmod(s, O_BLOCKS)
             y = y_pool.tile([P, PIXELS], F32, name="y")
             for t in range(PIXEL_TILES):
-                nc.scalar.activation(
-                    out=y[:, t * N_TILE : (t + 1) * N_TILE],
-                    in_=banks[n, b, t][:],
-                    func=ACT.Identity,
-                    bias=bias_mean[:, b : b + 1],
-                )
+                if on_vector:
+                    nc.vector.tensor_scalar_add(
+                        out=y[:, t * N_TILE : (t + 1) * N_TILE],
+                        in0=banks[n, b, t][:],
+                        scalar1=bias_mean[:, b : b + 1],
+                    )
+                else:
+                    nc.scalar.activation(
+                        out=y[:, t * N_TILE : (t + 1) * N_TILE],
+                        in_=banks[n, b, t][:],
+                        func=ACT.Identity,
+                        bias=bias_mean[:, b : b + 1],
+                    )
             nc.sync.dma_start(out=y_rows[n, b], in_=y[:])
 
         bias_rows = const.tile([P, COUT], BF16)
@@ -197,11 +205,16 @@ def tile_conv_1x1_9_layer_t_kernel(tc, x, weights, biases, out):
 
         y_pool = ctx.enter_context(tc.tile_pool(name="y_pool", bufs=Y_BUFS))
 
-        for u in range(2, UNITS + EMPTY_LAG):
-            if u < UNITS:
-                regroup_unit(u)
-            if u - 1 < UNITS:
-                quantise_unit(u - 1)
-                multiply_unit(u - 1)
+        for u in range(2, UNITS):
+            regroup_unit(u)
+            quantise_unit(u - 1)
+            multiply_unit(u - 1)
             if u >= EMPTY_LAG:
                 empty_block(u - EMPTY_LAG)
+
+        for t in range(PIXEL_TILES):
+            quantise_unit(UNITS - 1, t * N_TILE, N_TILE)
+            multiply_unit(UNITS - 1, [t])
+        empty_block(UNITS - 3)
+        empty_block(UNITS - 2)
+        empty_block(UNITS - 1, on_vector=True)

@@ -27,7 +27,7 @@ RUN = 4
 VECTOR_RUNS = 168
 VECTOR_LAYERS = 3
 RAW_BUFS = 12
-Y_BUFS = 12
+Y_BUFS = 6
 EMPTY_LAG = 3
 
 FLOPS = 2 * IMAGES * PIXELS * CIN * COUT
@@ -37,7 +37,7 @@ def tile_conv_1x1_9_layer_t_kernel(tc, x, weights, biases, out):
     nc = tc.nc
     assert O_BLOCKS == PASSES
     w_rows = weights.rearrange("i (m b) c s t -> i m b (c s t)", b=O_BLOCKS)
-    y_rows = out.rearrange("n (m b) h v -> n b m (h v)", b=O_BLOCKS)
+    y_rows = out.rearrange("n (m b) h v -> n m b (h v)", b=O_BLOCKS)
 
     with ExitStack() as ctx:
         ctx.enter_context(tc.manual_schedule())
@@ -52,6 +52,7 @@ def tile_conv_1x1_9_layer_t_kernel(tc, x, weights, biases, out):
         x_codes = {}
         x_scales = {}
         banks = {}
+        y_images = {}
 
         def load_unit(u):
             n, g = divmod(u, PASSES)
@@ -102,7 +103,9 @@ def tile_conv_1x1_9_layer_t_kernel(tc, x, weights, biases, out):
 
         def empty_block(s, on_vector=False):
             n, b = divmod(s, O_BLOCKS)
-            y = y_pool.tile([P, PIXELS], F32, name="y")
+            if b == 0:
+                y_images[n] = y_pool.tile([P, O_BLOCKS, PIXELS], F32, name="y")
+            y = y_images[n][:, b, :]
             for t in range(PIXEL_TILES):
                 if on_vector:
                     nc.vector.tensor_scalar_add(
@@ -117,7 +120,8 @@ def tile_conv_1x1_9_layer_t_kernel(tc, x, weights, biases, out):
                         func=ACT.Identity,
                         bias=bias_mean[:, b : b + 1],
                     )
-            nc.sync.dma_start(out=y_rows[n, b], in_=y[:])
+            if b == O_BLOCKS - 1:
+                nc.sync.dma_start(out=y_rows[n], in_=y_images[n][:])
 
         bias_rows = const.tile([P, COUT], BF16)
         nc.vector.memset(bias_rows[:], 0.0)

@@ -26,7 +26,7 @@ WORDS = PACK // 2
 RUN = 4
 VECTOR_RUNS = 168
 VECTOR_LAYERS = 3
-RAW_BUFS = 12
+RAW_BUFS = 6
 Y_BUFS = 6
 EMPTY_LAG = 3
 
@@ -54,22 +54,24 @@ def tile_conv_1x1_9_layer_t_kernel(tc, x, weights, biases, out):
         banks = {}
         y_images = {}
 
-        def load_unit(u):
-            n, g = divmod(u, PASSES)
-            raw = raw_pool.tile([P, PACK, PIXELS], BF16, name="raw")
-            rows = x[n].rearrange("(g p j) h v -> g p j (h v)", g=PASSES, p=P, j=PACK)
-            nc.sync.dma_start(out=raw[:], in_=rows[g])
-            x_raw[u] = raw
+        def load_image(n, pieces=1):
+            raw = raw_pool.tile([P, PASSES, PACK * PIXELS], BF16, name="raw")
+            rows = x[n].rearrange("(g p j) h v -> p g (j h v)", g=PASSES, p=P, j=PACK)
+            step = PASSES // pieces
+            for g in range(0, PASSES, step):
+                nc.sync.dma_start(out=raw[:, g : g + step, :], in_=rows[:, g : g + step, :])
+            x_raw[n] = raw
 
         def regroup_unit(u):
+            n, g = divmod(u, PASSES)
             grouped = grouped_pool.tile([P, PIXELS, PACK], BF16, name="grouped", align_bytes=64)
-            src = x_raw[u][:].rearrange("p j (r i) -> p r j i", i=RUN)
+            src = x_raw[n][:, g, :].rearrange("p (j r i) -> p r j i", j=PACK, i=RUN)
             dst = grouped[:].rearrange("p (r i) j -> p r j i", i=RUN)
             nc.vector.tensor_copy(out=dst[:, 0:VECTOR_RUNS], in_=src[:, 0:VECTOR_RUNS])
             nc.scalar.copy(out=dst[:, VECTOR_RUNS:], in_=src[:, VECTOR_RUNS:])
             x_grouped[u] = grouped
-            if u + RAW_BUFS < UNITS:
-                load_unit(u + RAW_BUFS)
+            if g == PASSES - 1 and n + RAW_BUFS < IMAGES:
+                load_image(n + RAW_BUFS)
 
         def quantise_unit(u, first_pixel=0, pixel_count=PIXELS):
             n, g = divmod(u, PASSES)
@@ -139,8 +141,9 @@ def tile_conv_1x1_9_layer_t_kernel(tc, x, weights, biases, out):
                 w_layer = w_pool.tile([P, O_BLOCKS, CIN], BF16, name="w_layer%d" % i)
                 nc.sync.dma_start(out=w_layer[:], in_=w_rows[i])
                 w_layers.append(w_layer)
-            for u in range(RAW_BUFS):
-                load_unit(u)
+            load_image(0, pieces=PASSES)
+            for n in range(1, RAW_BUFS):
+                load_image(n)
 
             w_sum = w_pool.tile([P, O_BLOCKS, CIN], F32)
             for i in range(1, VECTOR_LAYERS):

@@ -27,6 +27,7 @@ RUN = 4
 VECTOR_RUNS = 168
 VECTOR_LAYERS = 3
 RAW_BUFS = 6
+DMA_ALIGN = 256
 Y_BUFS = 6
 EMPTY_LAG = 3
 
@@ -55,7 +56,7 @@ def tile_conv_1x1_9_layer_t_kernel(tc, x, weights, biases, out):
         y_images = {}
 
         def load_image(n, pieces=1):
-            raw = raw_pool.tile([P, PASSES, PACK * PIXELS], BF16, name="raw")
+            raw = raw_pool.tile([P, PASSES, PACK * PIXELS], BF16, name="raw", align_bytes=DMA_ALIGN)
             rows = x[n].rearrange("(g p j) h v -> p g (j h v)", g=PASSES, p=P, j=PACK)
             step = PASSES // pieces
             for g in range(0, PASSES, step):
@@ -106,7 +107,7 @@ def tile_conv_1x1_9_layer_t_kernel(tc, x, weights, biases, out):
         def empty_block(s, on_vector=False):
             n, b = divmod(s, O_BLOCKS)
             if b == 0:
-                y_images[n] = y_pool.tile([P, O_BLOCKS, PIXELS], F32, name="y")
+                y_images[n] = y_pool.tile([P, O_BLOCKS, PIXELS], F32, name="y", align_bytes=DMA_ALIGN)
             y = y_images[n][:, b, :]
             for t in range(PIXEL_TILES):
                 if on_vector:
@@ -138,7 +139,7 @@ def tile_conv_1x1_9_layer_t_kernel(tc, x, weights, biases, out):
         with tc.tile_pool(name="w_pool", bufs=1) as w_pool:
             w_layers = []
             for i in range(LAYERS):
-                w_layer = w_pool.tile([P, O_BLOCKS, CIN], BF16, name="w_layer%d" % i)
+                w_layer = w_pool.tile([P, O_BLOCKS, CIN], BF16, name="w_layer%d" % i, align_bytes=DMA_ALIGN)
                 nc.sync.dma_start(out=w_layer[:], in_=w_rows[i])
                 w_layers.append(w_layer)
             load_image(0, pieces=PASSES)

@@ -28,6 +28,7 @@ VECTOR_RUNS = 168
 VECTOR_LAYERS = 3
 RAW_BUFS = 6
 DMA_ALIGN = 256
+BLOCK_STORE_IMAGES = 2
 Y_BUFS = 6
 EMPTY_LAG = 3
 
@@ -123,7 +124,9 @@ def tile_conv_1x1_9_layer_t_kernel(tc, x, weights, biases, out):
                         func=ACT.Identity,
                         bias=bias_mean[:, b : b + 1],
                     )
-            if b == O_BLOCKS - 1:
+            if n >= IMAGES - BLOCK_STORE_IMAGES:
+                nc.sync.dma_start(out=y_rows[n][:, b, :], in_=y)
+            elif b == O_BLOCKS - 1:
                 nc.sync.dma_start(out=y_rows[n], in_=y_images[n][:])
 
         bias_rows = const.tile([P, COUT], BF16)

from contextlib import ExitStack

import concourse.mybir as mybir
from concourse.masks import make_identity

F32 = mybir.dt.float32
BF16 = mybir.dt.bfloat16
U32 = mybir.dt.uint32
U8 = mybir.dt.uint8
FP8X4 = mybir.dt.float8_e4m3fn_x4
ADD = mybir.AluOpType.add
ACT = mybir.ActivationFunctionType

P = 128
PACK = 4
K_PASS = P * PACK
N_TILE = 512

IMAGES, CIN, PIXELS, COUT, LAYERS = 8, 1024, 32 * 32, 256, 9
PASSES = CIN // K_PASS
O_BLOCKS = COUT // P
PIXEL_TILES = PIXELS // N_TILE
UNITS = IMAGES * PASSES
WORDS = PACK // 2

RUN = 4
VECTOR_RUNS = 168
VECTOR_LAYERS = 3
RAW_BUFS = 6
DMA_ALIGN = 256
BLOCK_STORE_IMAGES = 2
Y_BUFS = 6
EMPTY_LAG = 3

FLOPS = 2 * IMAGES * PIXELS * CIN * COUT


def tile_conv_1x1_9_layer_t_kernel(tc, x, weights, biases, out):
    nc = tc.nc
    assert O_BLOCKS == PASSES
    w_rows = weights.rearrange("i (m b) c s t -> i m b (c s t)", b=O_BLOCKS)
    y_rows = out.rearrange("n (m b) h v -> n m b (h v)", b=O_BLOCKS)

    with ExitStack() as ctx:
        ctx.enter_context(tc.manual_schedule())
        const = ctx.enter_context(tc.tile_pool(name="const", bufs=1))
        raw_pool = ctx.enter_context(tc.tile_pool(name="raw_pool", bufs=RAW_BUFS))
        grouped_pool = ctx.enter_context(tc.tile_pool(name="grouped_pool", bufs=3))
        code_pool = ctx.enter_context(tc.tile_pool(name="code_pool", bufs=3))
        psum = ctx.enter_context(tc.psum_pool(name="psum", bufs=8))

        x_raw = {}
        x_grouped = {}
        x_codes = {}
        x_scales = {}
        banks = {}
        y_images = {}

        def load_image(n, pieces=1):
            raw = raw_pool.tile([P, PASSES, PACK * PIXELS], BF16, name="raw", align_bytes=DMA_ALIGN)
            rows = x[n].rearrange("(g p j) h v -> p g (j h v)", g=PASSES, p=P, j=PACK)
            step = PASSES // pieces
            for g in range(0, PASSES, step):
                nc.sync.dma_start(out=raw[:, g : g + step, :], in_=rows[:, g : g + step, :])
            x_raw[n] = raw

        def regroup_unit(u):
            n, g = divmod(u, PASSES)
            grouped = grouped_pool.tile([P, PIXELS, PACK], BF16, name="grouped", align_bytes=64)
            src = x_raw[n][:, g, :].rearrange("p (j r i) -> p r j i", j=PACK, i=RUN)
            dst = grouped[:].rearrange("p (r i) j -> p r j i", i=RUN)
            nc.vector.tensor_copy(out=dst[:, 0:VECTOR_RUNS], in_=src[:, 0:VECTOR_RUNS])
            nc.scalar.copy(out=dst[:, VECTOR_RUNS:], in_=src[:, VECTOR_RUNS:])
            x_grouped[u] = grouped
            if g == PASSES - 1 and n + RAW_BUFS < IMAGES:
                load_image(n + RAW_BUFS)

        def quantise_unit(u, first_pixel=0, pixel_count=PIXELS):
            n, g = divmod(u, PASSES)
            if g == 0:
                x_codes[n] = code_pool.tile([P, PASSES, PIXELS], U32, name="codes", align_bytes=64)
                x_scales[n] = code_pool.tile([P, PASSES, PIXELS], U8, name="scales", align_bytes=64)
            pixels = slice(first_pixel, first_pixel + pixel_count)
            nc.vector.quantize_mx(
                out=x_codes[n][:, g, pixels].bitcast(FP8X4),
                scales=x_scales[n][:, g, pixels],
                in_=x_grouped[u][:, pixels, :].rearrange("p w j -> p (w j)"),
            )

        def multiply_unit(u, pixel_tiles=range(PIXEL_TILES)):
            n, g = divmod(u, PASSES)
            for t in pixel_tiles:
                pixels = slice(t * N_TILE, (t + 1) * N_TILE)
                for b in range(O_BLOCKS):
                    o_cols = slice((g * O_BLOCKS + b) * P, (g * O_BLOCKS + b + 1) * P)
                    if g == 0:
                        banks[n, b, t] = psum.tile([P, N_TILE], F32, tag="bank", name="acc")
                    nc.tensor.matmul_mx(
                        out=banks[n, b, t][:],
                        lhsT=w_codes[:, o_cols].bitcast(FP8X4),
                        lhsT_scale=w_scales[:, o_cols],
                        rhs=x_codes[n][:, g, pixels].bitcast(FP8X4),
                        rhs_scale=x_scales[n][:, g, pixels],
                        start=(g == 0),
                        stop=(g == PASSES - 1),
                    )

        def empty_block(s, on_vector=False):
            n, b = divmod(s, O_BLOCKS)
            if b == 0:
                y_images[n] = y_pool.tile([P, O_BLOCKS, PIXELS], F32, name="y", align_bytes=DMA_ALIGN)
            y = y_images[n][:, b, :]
            for t in range(PIXEL_TILES):
                if on_vector:
                    nc.vector.tensor_scalar_add(
                        out=y[:, t * N_TILE : (t + 1) * N_TILE],
                        in0=banks[n, b, t][:],
                        scalar1=bias_mean[:, b : b + 1],
                    )
                else:
                    nc.scalar.activation(
                        out=y[:, t * N_TILE : (t + 1) * N_TILE],
                        in_=banks[n, b, t][:],
                        func=ACT.Identity,
                        bias=bias_mean[:, b : b + 1],
                    )
            if n >= IMAGES - BLOCK_STORE_IMAGES:
                nc.sync.dma_start(out=y_rows[n][:, b, :], in_=y)
            elif b == O_BLOCKS - 1:
                nc.sync.dma_start(out=y_rows[n], in_=y_images[n][:])

        bias_rows = const.tile([P, COUT], BF16)
        nc.vector.memset(bias_rows[:], 0.0)
        nc.scalar.dma_start(out=bias_rows[0:LAYERS, :], in_=biases)
        ident = const.tile([P, P], F32)
        make_identity(nc, ident[:])
        ident_bf = const.tile([P, P], BF16)
        make_identity(nc, ident_bf[:])
        w_codes = const.tile([P, PASSES * O_BLOCKS * P], U32, align_bytes=64)
        w_scales = const.tile([P, PASSES * O_BLOCKS * P], U8, align_bytes=64)

        with tc.tile_pool(name="w_pool", bufs=1) as w_pool:
            w_layers = []
            for i in range(LAYERS):
                w_layer = w_pool.tile([P, O_BLOCKS, CIN], BF16, name="w_layer%d" % i, align_bytes=DMA_ALIGN)
                nc.sync.dma_start(out=w_layer[:], in_=w_rows[i])
                w_layers.append(w_layer)
            load_image(0, pieces=PASSES)
            for n in range(1, RAW_BUFS):
                load_image(n)

            w_sum = w_pool.tile([P, O_BLOCKS, CIN], F32)
            for i in range(1, VECTOR_LAYERS):
                for b in range(O_BLOCKS):
                    so_far = w_layers[0] if i == 1 else w_sum
                    nc.vector.tensor_tensor(
                        out=w_sum[:, b, :], in0=so_far[:, b, :], in1=w_layers[i][:, b, :], op=ADD
                    )
            w_banks = {}
            for i in range(VECTOR_LAYERS, LAYERS):
                for g in range(PASSES):
                    for b in range(O_BLOCKS):
                        if i == VECTOR_LAYERS:
                            w_banks[g, b] = psum.tile([P, K_PASS], F32, tag="bank", name="w_bank")
                        nc.tensor.matmul(
                            out=w_banks[g, b][:],
                            lhsT=ident_bf[:],
                            rhs=w_layers[i][:, b, g * K_PASS : (g + 1) * K_PASS],
                            start=(i == VECTOR_LAYERS),
                            stop=(i == LAYERS - 1),
                        )
            w_mean = w_pool.tile([P, O_BLOCKS, CIN], BF16)
            for g in range(PASSES):
                for b in range(O_BLOCKS):
                    channels = slice(g * K_PASS, (g + 1) * K_PASS)
                    nc.vector.tensor_tensor(
                        out=w_sum[:, b, channels], in0=w_banks[g, b][:], in1=w_sum[:, b, channels], op=ADD
                    )
                    nc.scalar.activation(
                        out=w_mean[:, b, channels], in_=w_sum[:, b, channels], func=ACT.Copy, scale=1.0 / LAYERS
                    )

            regroup_unit(0)

            w_grouped = w_pool.tile([P, PASSES * O_BLOCKS * P * PACK], BF16, align_bytes=64)
            w_grouped_words = w_grouped[:].bitcast(F32).rearrange(
                "p (g b m e) -> p g b m e", g=PASSES, b=O_BLOCKS, e=WORDS
            )
            pass_words = K_PASS // 2
            for g in range(PASSES):
                w_t = psum.tile([P, O_BLOCKS, WORDS, P], F32, tag="bank")
                for b in range(O_BLOCKS):
                    words = w_mean[:, b, :].bitcast(F32)
                    for e in range(WORDS):
                        nc.tensor.transpose(
                            w_t[:, b, e, :], words[:, g * pass_words + e : (g + 1) * pass_words : WORDS], ident[:]
                        )
                nc.scalar.copy(out=w_grouped_words[:, g], in_=w_t[:].rearrange("p b e m -> p b m e"))

            regroup_unit(1)
            quantise_unit(0)
            nc.vector.quantize_mx(out=w_codes[:].bitcast(FP8X4), scales=w_scales[:], in_=w_grouped[:])
            bias_t = psum.tile([P, P], F32, tag="bank")
            nc.tensor.transpose(bias_t[:], bias_rows[:].bitcast(F32), ident[:])
            bias_sum = const.tile([P, O_BLOCKS], F32)
            nc.vector.tensor_reduce(
                out=bias_sum[:],
                in_=bias_t[:].bitcast(BF16).rearrange("m (i b) -> m b i", b=O_BLOCKS)[:, :, 0:LAYERS],
                axis=mybir.AxisListType.X,
                op=ADD,
            )
            bias_mean = const.tile([P, O_BLOCKS], F32)
            nc.vector.tensor_scalar_mul(out=bias_mean[:], in0=bias_sum[:], scalar1=1.0 / LAYERS)

            multiply_unit(0)

        y_pool = ctx.enter_context(tc.tile_pool(name="y_pool", bufs=Y_BUFS))

        for u in range(2, UNITS):
            regroup_unit(u)
            quantise_unit(u - 1)
            multiply_unit(u - 1)
            if u >= EMPTY_LAG:
                empty_block(u - EMPTY_LAG)

        for t in range(PIXEL_TILES):
            quantise_unit(UNITS - 1, t * N_TILE, N_TILE)
            multiply_unit(UNITS - 1, [t])
        empty_block(UNITS - 3)
        empty_block(UNITS - 2)
        empty_block(UNITS - 1, on_vector=True)
